import numpy as np
import ml_dtypes


def mxq(x, axis, fmt="e4m3"):
    dtype, down = {"e4m3": (ml_dtypes.float8_e4m3fn, 7), "e5m2": (ml_dtypes.float8_e5m2, 14)}[fmt]
    v = np.moveaxis(np.asarray(x, np.float32).astype(ml_dtypes.bfloat16).astype(np.float64), axis, -1)
    blocks = v.reshape(v.shape[:-1] + (-1, 32))
    amax = np.abs(blocks).max(-1, keepdims=True)
    byte = np.maximum(np.where(amax > 0, np.frexp(amax)[1] - 1 + 127, 0) - down, 1)
    scale = np.exp2(byte - 127.0)
    codes = (blocks / scale).astype(np.float32).astype(dtype).astype(np.float64)
    return np.moveaxis((codes * scale).reshape(v.shape), -1, axis)


WIDE = False


def mx_kscale(k):
    if not WIDE:
        return np.ones(k)
    levels = np.array([10, -10, 5, -5, 0])
    if k % 512:
        return np.exp2(np.random.permutation(np.resize(levels, k // 32))).repeat(32)
    a = np.empty((k // 512, 16))
    for p in range(k // 512):
        a[p, :8] = np.random.permutation(np.resize(levels, 8))
        for g in range(8):
            far = levels[np.abs(levels - a[p, g]) >= 10]
            a[p, g + 8] = far[np.random.randint(len(far))]
    return np.exp2(a.ravel()).repeat(32)


BF16 = ml_dtypes.bfloat16


def bf(x):
    return np.asarray(x, np.float32).astype(BF16)


def f64(x):
    return np.asarray(x).astype(np.float64)


B, S, E, H, D = 2, 512, 512, 4, 512


def setup_inputs():
    s = mx_kscale(E)
    ckv = 0.75 * D ** 0.25 / np.sqrt(E)
    cq = 3.0 / np.sqrt(E)
    return {"x": bf(np.random.standard_normal((B, S, E)) * s),
            "Wq": bf(np.random.standard_normal((E, H * D)) * cq / s[:, None]),
            "bq": bf(np.random.standard_normal(H * D) * 0.25),
            "Wk": bf(np.random.standard_normal((E, H * D)) * ckv / s[:, None]),
            "bk": bf(np.random.standard_normal(H * D)),
            "Wv": bf(np.random.standard_normal((E, H * D)) * ckv / s[:, None]),
            "bv": bf(np.random.standard_normal(H * D))}


def reference(x, Wq, bq, Wk, bk, Wv, bv):
    xq = mxq(f64(x), 2, "e4m3")

    def proj(W, bias):
        y = (xq @ mxq(f64(W), 0, "e4m3")) + f64(bias)
        return y.reshape(B, S, H, D).transpose(0, 2, 1, 3)

    q = proj(Wq, bq)
    k = proj(Wk, bk)
    v = proj(Wv, bv)
    kv = k * np.swapaxes(v, -1, -2) * (1.0 / np.sqrt(D))
    e = np.exp(kv - kv.max(axis=2, keepdims=True))
    attn = e / e.sum(axis=2, keepdims=True)
    return np.sum(attn * q, axis=2)

@@ -1,0 +1,357 @@
+from contextlib import ExitStack
+import math
+
+import concourse.masks as masks
+import concourse.mybir as mybir
+
+BF16 = mybir.dt.bfloat16
+F32 = mybir.dt.float32
+U32 = mybir.dt.uint32
+U8 = mybir.dt.uint8
+FP8X4 = mybir.dt.float8_e4m3fn_x4
+ALU = mybir.AluOpType
+ACT = mybir.ActivationFunctionType
+
+P = 128
+PACK = 4
+B, S, E, H, D = 2, 512, 512, 4, 512
+assert E == P * PACK and S == D
+
+J_TILES = D // P
+TILES_PER_HEAD = B * J_TILES
+N_TILES = H * TILES_PER_HEAD
+TOKEN_TILES = S // P
+HALF_E = E // 2
+
+BLOCKS = ("k", "v", "q")
+BLOCK_COL = {"k": 0, "v": D, "q": 2 * D}
+HEAD_COLS = 3 * D
+HALF_D = D // 2
+
+RUN = 4
+STEP_COLS = HEAD_COLS // TILES_PER_HEAD
+
+MAX_LAG = 2
+EXP_LAG = 3
+SUM_LAG = 4
+
+FLOPS = 2 * B * S * E * 3 * H * D
+
+
+def tile_multihead_attention_pa_kernel(tc, x, Wq, bq, Wk, bk, Wv, bv, out):
+    nc = tc.nc
+    weights = {"q": Wq, "k": Wk, "v": Wv}
+    score_scale = 1.0 / math.sqrt(D)
+    n_bias_rows = H * J_TILES
+
+    with ExitStack() as ctx:
+        keep = ctx.enter_context(tc.tile_pool(name="keep", bufs=1))
+        group_pool = ctx.enter_context(tc.tile_pool(name="group", bufs=2))
+        work = ctx.enter_context(tc.tile_pool(name="work", bufs=3))
+        psum = ctx.enter_context(tc.psum_pool(name="psum", bufs=2))
+        ctx.enter_context(tc.manual_schedule())
+
+        x_raw = keep.tile([P, B * TOKEN_TILES * E], BF16)
+        x_grouped = keep.tile([P, B * S * PACK], BF16, align_bytes=64)
+        x_codes = keep.tile([P, B * S], U32, align_bytes=64)
+        x_scales = keep.tile([P, B * S], U8, align_bytes=64)
+        raw = {}
+        codes = {}
+        scales = {}
+        grouped = {}
+        for head in range(H):
+            for which in BLOCKS:
+                raw[(which, head)] = keep.tile([P, PACK, D], BF16, name="raw_%s%d" % (which, head))
+            codes[head] = keep.tile([P, HEAD_COLS], U32, name="codes%d" % head, align_bytes=64)
+            scales[head] = keep.tile([P, HEAD_COLS], U8, name="scales%d" % head, align_bytes=64)
+
+        identity = keep.tile([P, P], F32)
+        identity_bf = keep.tile([P, P], BF16)
+        n_stage_rows = 2 * n_bias_rows + J_TILES
+        bias_rows = keep.tile([P, P], BF16)
+        neg_bk = keep.tile([P, n_bias_rows], F32)
+        bq_cols = keep.tile([P, n_bias_rows], F32)
+        bv0_cols = keep.tile([P, J_TILES], BF16)
+        bv_all = keep.tile([P, H * D], BF16)
+        zero_col = keep.tile([P, 1], F32)
+        table_warm = keep.tile([P, 1], F32)
+        neg_max = keep.tile([P, N_TILES], F32)
+        denominator = keep.tile([P, N_TILES], F32)
+        numerator = keep.tile([P, N_TILES], F32)
+        reciprocal = keep.tile([P, N_TILES], F32)
+        result = keep.tile([P, P], F32)
+        result_rows = keep.tile([N_TILES, P], F32)
+        products = keep.tile([P, S], F32)
+
+        def load_x(batch):
+            first = batch * TOKEN_TILES * E
+            nc.sync.dma_start(
+                out=x_raw[:, first : first + TOKEN_TILES * E].rearrange("p (n e) -> p n e", e=E),
+                in_=x[batch].rearrange("(n p) e -> p n e", p=P),
+            )
+
+        def load_weight_block(which, head):
+            nc.sync.dma_start(
+                out=raw[(which, head)][:],
+                in_=weights[which][:, head * D : (head + 1) * D].rearrange("(p t) c -> p t c", t=PACK),
+            )
+
+        def load_bv(head):
+            cols = slice(head * D, (head + 1) * D)
+            nc.sync.dma_start(out=bv_all[:, cols], in_=bv[cols].partition_broadcast(P))
+
+        load_weight_block("v", 0)
+        load_x(0)
+        load_weight_block("k", 0)
+        load_weight_block("q", 0)
+        load_weight_block("k", 1)
+        load_x(1)
+        load_weight_block("v", 1)
+        load_weight_block("q", 1)
+        load_bv(1)
+        for head in range(2, H):
+            for which in ("k", "v", "q"):
+                load_weight_block(which, head)
+            load_bv(head)
+
+        nc.vector.memset(bias_rows[:], 0.0)
+        nc.scalar.dma_start(out=bias_rows[0:n_bias_rows, :], in_=bk.rearrange("(r p) -> r p", p=P))
+        nc.scalar.dma_start(out=bias_rows[n_bias_rows : 2 * n_bias_rows, :], in_=bq.rearrange("(r p) -> r p", p=P))
+        nc.scalar.dma_start(out=bias_rows[2 * n_bias_rows : n_stage_rows, :], in_=bv[0:D].rearrange("(r p) -> r p", p=P))
+
+        masks.make_identity(nc, identity[:])
+        nc.vector.memset(zero_col[:], 0.0)
+        nc.vector.memset(result[:], 0.0)
+        nc.vector.tensor_copy(out=identity_bf[:], in_=identity[:])
+        nc.scalar.activation(out=table_warm[:], in_=zero_col[:], func=ACT.Exp)
+
+        def quantise(in_, codes_out, scales_out):
+            nc.vector.quantize_mx(out=codes_out.bitcast(FP8X4), scales=scales_out, in_=in_)
+
+        def x_job(batch):
+            return (
+                x_grouped[:, batch * S * PACK : (batch + 1) * S * PACK],
+                x_codes[:, batch * S : (batch + 1) * S],
+                x_scales[:, batch * S : (batch + 1) * S],
+            )
+
+        def weight_job(head, first_col, n_cols):
+            cols = slice(first_col, first_col + n_cols)
+            return (grouped[head][:, cols, :].rearrange("p c t -> p (c t)"), codes[head][:, cols], scales[head][:, cols])
+
+        def transpose_x(batch):
+            x_words = x_raw[:].bitcast(F32)
+            grouped_words = x_grouped[:].bitcast(F32)
+            for pair in range(TOKEN_TILES // 2):
+                turned = psum.tile([P, 2, 2 * P], F32, tag="misc")
+                for block in range(2):
+                    n = batch * TOKEN_TILES + 2 * pair + block
+                    for u in range(2):
+                        words = x_words[:, n * HALF_E + u : (n + 1) * HALF_E : 2]
+                        nc.tensor.transpose(turned[:, u, block * P : (block + 1) * P], words, identity[:])
+                first_token = batch * S + pair * 2 * P
+                nc.scalar.copy(
+                    out=grouped_words[:, 2 * first_token : 2 * (first_token + 2 * P)].rearrange(
+                        "p (r u) -> p r u", u=2
+                    ),
+                    in_=turned[:].rearrange("p u r -> p r u"),
+                )
+
+        def new_grouped(head):
+            grouped[head] = group_pool.tile([P, HEAD_COLS, PACK], BF16, name="grouped", align_bytes=64)
+
+        def regroup(copy, head, first_col, n_cols):
+            for block, which in enumerate(BLOCKS):
+                lo = max(first_col, block * D)
+                hi = min(first_col + n_cols, (block + 1) * D)
+                if lo < hi:
+                    copy(
+                        out=grouped[head][:, lo:hi, :].rearrange("p (c i) t -> p c t i", i=RUN),
+                        in_=raw[(which, head)][:, :, lo - block * D : hi - block * D].rearrange(
+                            "p t (c i) -> p c t i", i=RUN
+                        ),
+                    )
+
+        last_period = N_TILES + SUM_LAG
+        to_quantise = {n: [] for n in range(last_period)}
+
+        def regroup_next_head(period):
+            if not 0 <= period < (H - 1) * TILES_PER_HEAD:
+                return
+            head, step = divmod(period, TILES_PER_HEAD)
+            head += 1
+            if step == 0:
+                new_grouped(head)
+            regroup(nc.scalar.copy, head, step * STEP_COLS, STEP_COLS)
+            for first_col, n_cols in ((BLOCK_COL["k"], 2 * D), (BLOCK_COL["q"], D)):
+                if step * STEP_COLS < first_col + n_cols <= (step + 1) * STEP_COLS:
+                    to_quantise[period + 1].append(weight_job(head, first_col, n_cols))
+
+        live = {}
+
+        def place(t):
+            head, rest = divmod(t, TILES_PER_HEAD)
+            batch, j_tile = divmod(rest, J_TILES)
+            return head, batch, j_tile
+
+        def out_row(t):
+            head, batch, j_tile = place(t)
+            return (batch * H + head) * J_TILES + j_tile
+
+        def project(name, t, stationary, stationary_cols, moving, moving_cols):
+            bank = psum.tile([P, S], F32, name=name + "_ps", tag=name)
+            nc.tensor.matmul_mx(
+                out=bank[:],
+                lhsT=stationary[0][:, stationary_cols].bitcast(FP8X4),
+                lhsT_scale=stationary[1][:, stationary_cols],
+                rhs=moving[0][:, moving_cols].bitcast(FP8X4),
+                rhs_scale=moving[1][:, moving_cols],
+                start=True,
+                stop=True,
+            )
+            live[(name, t)] = bank
+
+        def project_features(name, t):
+            head, batch, j_tile = place(t)
+            first = BLOCK_COL[name] + j_tile * P
+            project(
+                name, t, (codes[head], scales[head]), slice(first, first + P),
+                (x_codes, x_scales), slice(batch * S, (batch + 1) * S),
+            )
+
+        def project_k_and_v(t):
+            if not 0 <= t < N_TILES:
+                return
+            head, batch, j_tile = place(t)
+            project_features("k", t)
+            first = batch * S + j_tile * P
+            project(
+                "v", t, (x_codes, x_scales), slice(first, first + P),
+                (codes[head], scales[head]), slice(BLOCK_COL["v"], BLOCK_COL["v"] + D),
+            )
+
+        def project_q(t):
+            if not 0 <= t < N_TILES:
+                return
+            project_features("q", t)
+
+        def finish_k(t):
+            if not 0 <= t < N_TILES:
+                return
+            head, batch, j_tile = place(t)
+            bias_col = head * J_TILES + j_tile
+            neg_k = work.tile([P, S], F32, name="neg_k")
+            nc.scalar.activation(
+                out=neg_k[:],
+                in_=live[("k", t)][:],
+                func=ACT.Identity,
+                bias=neg_bk[:, bias_col : bias_col + 1],
+                scale=-score_scale,
+            )
+            live[("neg_k", t)] = neg_k
+
+        def finish_v_and_multiply(t):
+            if not 0 <= t < N_TILES:
+                return
+            head, batch, j_tile = place(t)
+            v_full = work.tile([P, S], F32, name="v_full")
+            nc.vector.tensor_tensor(
+                out=v_full[:], in0=live[("v", t)][:], in1=bv_all[:, head * D : (head + 1) * D], op=ALU.add
+            )
+            live[("v_full", t)] = v_full
+            neg_score = work.tile([P, S], F32, name="neg_score", bufs=EXP_LAG + 2)
+            nc.gpsimd.tensor_tensor(out=neg_score[:], in0=live[("neg_k", t)][:], in1=live[("v_full", t)][:], op=ALU.mult)
+            live[("neg_score", t)] = neg_score
+
+        def row_maximum(t):
+            if not 0 <= t < N_TILES:
+                return
+            col = out_row(t)
+            nc.vector.tensor_reduce(
+                out=neg_max[:, col : col + 1], in_=live[("neg_score", t)][:], axis=mybir.AxisListType.X, op=ALU.min
+            )
+
+        def exponentials(t):
+            if not 0 <= t < N_TILES:
+                return
+            col = out_row(t)
+            weight = work.tile([P, S], F32, name="weight")
+            nc.scalar.activation(
+                out=weight[:],
+                in_=live[("neg_score", t)][:],
+                func=ACT.Exp,
+                bias=neg_max[:, col : col + 1],
+                scale=-1.0,
+                accum_out=denominator[:, col : col + 1],
+            )
+            live[("weight", t)] = weight
+
+        def weighted_sum(t):
+            if not 0 <= t < N_TILES:
+                return
+            head, batch, j_tile = place(t)
+            bias_col = head * J_TILES + j_tile
+            col = out_row(t)
+            nc.vector.scalar_tensor_tensor(
+                out=products[:],
+                in0=live[("q", t)][:],
+                scalar=bq_cols[:, bias_col : bias_col + 1],
+                in1=live[("weight", t)][:],
+                op0=ALU.add,
+                op1=ALU.mult,
+                accum_out=numerator[:, col : col + 1],
+            )
+
+        transpose_x(0)
+        bias_cols = psum.tile([P, P], BF16, tag="misc")
+        nc.tensor.transpose(bias_cols[:], bias_rows[:], identity_bf[:])
+        nc.scalar.mul(out=neg_bk[:], in_=bias_cols[:, 0:n_bias_rows], mul=-score_scale)
+        nc.scalar.copy(out=bq_cols[:], in_=bias_cols[:, n_bias_rows : 2 * n_bias_rows])
+        nc.scalar.copy(out=bv0_cols[:], in_=bias_cols[:, 2 * n_bias_rows : n_stage_rows])
+        spread = psum.tile([P, D], F32, tag="misc")
+        for r in range(J_TILES):
+            nc.tensor.matmul(
+                out=spread[:, r * P : (r + 1) * P],
+                lhsT=bv0_cols[:, r : r + 1].to_broadcast([P, P]),
+                rhs=identity_bf[:],
+                start=True,
+                stop=True,
+            )
+        nc.scalar.copy(out=bv_all[:, 0:D], in_=spread[:])
+        new_grouped(0)
+        regroup(nc.vector.tensor_copy, 0, BLOCK_COL["v"], D)
+        quantise(*weight_job(0, BLOCK_COL["v"], D))
+        regroup(nc.vector.tensor_copy, 0, BLOCK_COL["k"], HALF_D)
+        quantise(*x_job(0))
+        quantise(*weight_job(0, BLOCK_COL["k"], HALF_D))
+        head0_rest = [BLOCK_COL["k"] + HALF_D, BLOCK_COL["q"], BLOCK_COL["q"] + HALF_D]
+
+        for period in range(-1, last_period):
+            bias_last = period >= 0 and len(to_quantise[period]) > 0
+            project_q(period - SUM_LAG + 1)
+            project_k_and_v(period + 1)
+            finish_k(period)
+            if not bias_last:
+                finish_v_and_multiply(period)
+            if 0 <= period < len(head0_rest):
+                regroup(nc.vector.tensor_copy, 0, head0_rest[period], HALF_D)
+                to_quantise[period].append(weight_job(0, head0_rest[period], HALF_D))
+            if period == 1:
+                transpose_x(1)
+                to_quantise[period + 1].append(x_job(1))
+            regroup_next_head(period)
+            row_maximum(period - MAX_LAG)
+            exponentials(period - EXP_LAG)
+            weighted_sum(period - SUM_LAG)
+            if period >= 0:
+                for job in to_quantise[period]:
+                    quantise(*job)
+            if bias_last:
+                finish_v_and_multiply(period)
+
+        nc.vector.reciprocal(out=reciprocal[:], in_=denominator[:])
+        nc.vector.tensor_tensor(out=result[:, 0:N_TILES], in0=numerator[:], in1=reciprocal[:], op=ALU.mult)
+        turned_result = psum.tile([P, P], F32, tag="misc")
+        nc.tensor.transpose(turned_result[:], result[:], identity[:])
+        nc.scalar.copy(out=result_rows[:], in_=turned_result[0:N_TILES, :])
+        nc.sync.dma_start(out=out.rearrange("b h (n p) -> (b h n) p", p=P), in_=result_rows[:])

@@ -29,11 +29,14 @@ HEAD_COLS = 3 * D
 HALF_D = D // 2
 
 RUN = 4
-STEP_COLS = HEAD_COLS // TILES_PER_HEAD
+BANK_COLS = 256
+MM_COLS = 128
+REGROUP_ORDER = ("v", "k", "q")
+FIRST_FILL = 1
 
 MAX_LAG = 2
-EXP_LAG = 3
-SUM_LAG = 4
+EXP_LAG = 2
+SUM_LAG = 3
 
 FLOPS = 2 * B * S * E * 3 * H * D
 
@@ -104,13 +107,9 @@ def tile_multihead_attention_pa_kernel(tc, x, Wq, bq, Wk, bk, Wv, bv, out):
         load_x(0)
         load_weight_block("k", 0)
         load_weight_block("q", 0)
-        load_weight_block("k", 1)
         load_x(1)
-        load_weight_block("v", 1)
-        load_weight_block("q", 1)
-        load_bv(1)
-        for head in range(2, H):
-            for which in ("k", "v", "q"):
+        for head in range(1, H):
+            for which in REGROUP_ORDER:
                 load_weight_block(which, head)
             load_bv(head)
 
@@ -175,17 +174,39 @@ def tile_multihead_attention_pa_kernel(tc, x, Wq, bq, Wk, bk, Wv, bv, out):
         last_period = N_TILES + SUM_LAG
         to_quantise = {n: [] for n in range(last_period)}
 
-        def regroup_next_head(period):
-            if not 0 <= period < (H - 1) * TILES_PER_HEAD:
+        fills = {}
+        for head in range(1, H):
+            banks = [(which, first) for which in REGROUP_ORDER for first in range(0, D, BANK_COLS)]
+            for step, (which, first) in enumerate(banks):
+                fills[(head - 1) * TILES_PER_HEAD + FIRST_FILL + step] = (head, which, first)
+        filled = {}
+
+        def fill_bank(period):
+            if period not in fills:
                 return
-            head, step = divmod(period, TILES_PER_HEAD)
-            head += 1
-            if step == 0:
+            head, which, first = fills[period]
+            bank = psum.tile([P, BANK_COLS * PACK], BF16, name="regroup_ps", tag="misc")
+            for c in range(0, BANK_COLS, MM_COLS):
+                nc.tensor.matmul(
+                    out=bank[:, c * PACK : (c + MM_COLS) * PACK].rearrange("p (c t) -> p c t", t=PACK),
+                    lhsT=identity_bf[:],
+                    rhs=raw[(which, head)][:, :, first + c : first + c + MM_COLS].rearrange("p t c -> p c t"),
+                    start=True,
+                    stop=True,
+                )
+            filled[period] = bank
+
+        def empty_bank(period):
+            if period - 1 not in fills:
+                return
+            head, which, first = fills[period - 1]
+            if head not in grouped:
                 new_grouped(head)
-            regroup(nc.scalar.copy, head, step * STEP_COLS, STEP_COLS)
-            for first_col, n_cols in ((BLOCK_COL["k"], 2 * D), (BLOCK_COL["q"], D)):
-                if step * STEP_COLS < first_col + n_cols <= (step + 1) * STEP_COLS:
-                    to_quantise[period + 1].append(weight_job(head, first_col, n_cols))
+            lo = BLOCK_COL[which] + first
+            words = grouped[head][:].rearrange("p c t -> p (c t)").bitcast(F32)
+            half = PACK // 2
+            nc.scalar.copy(out=words[:, lo * half : (lo + BANK_COLS) * half], in_=filled[period - 1][:].bitcast(F32))
+            to_quantise[period + 1].append(weight_job(head, lo, BANK_COLS))
 
         live = {}
 
@@ -327,27 +348,24 @@ def tile_multihead_attention_pa_kernel(tc, x, Wq, bq, Wk, bk, Wv, bv, out):
         head0_rest = [BLOCK_COL["k"] + HALF_D, BLOCK_COL["q"], BLOCK_COL["q"] + HALF_D]
 
         for period in range(-1, last_period):
-            bias_last = period >= 0 and len(to_quantise[period]) > 0
             project_q(period - SUM_LAG + 1)
             project_k_and_v(period + 1)
+            fill_bank(period)
             finish_k(period)
-            if not bias_last:
-                finish_v_and_multiply(period)
+            if period == 0:
+                transpose_x(1)
+                to_quantise[2].append(x_job(1))
             if 0 <= period < len(head0_rest):
                 regroup(nc.vector.tensor_copy, 0, head0_rest[period], HALF_D)
                 to_quantise[period].append(weight_job(0, head0_rest[period], HALF_D))
-            if period == 1:
-                transpose_x(1)
-                to_quantise[period + 1].append(x_job(1))
-            regroup_next_head(period)
+            empty_bank(period)
             row_maximum(period - MAX_LAG)
             exponentials(period - EXP_LAG)
             weighted_sum(period - SUM_LAG)
             if period >= 0:
                 for job in to_quantise[period]:
                     quantise(*job)
-            if bias_last:
-                finish_v_and_multiply(period)
+            finish_v_and_multiply(period)
 
         nc.vector.reciprocal(out=reciprocal[:], in_=denominator[:])
         nc.vector.tensor_tensor(out=result[:, 0:N_TILES], in0=numerator[:], in1=reciprocal[:], op=ALU.mult)

@@ -31,12 +31,11 @@ HALF_D = D // 2
 RUN = 4
 BANK_COLS = 256
 MM_COLS = 128
-REGROUP_ORDER = ("v", "k", "q")
-FIRST_FILL = 1
+FIRST_FILL = 2
 
-MAX_LAG = 2
+MAX_LAG = 1
 EXP_LAG = 2
-SUM_LAG = 3
+SUM_LAG = 2
 
 FLOPS = 2 * B * S * E * 3 * H * D
 
@@ -103,20 +102,19 @@ def tile_multihead_attention_pa_kernel(tc, x, Wq, bq, Wk, bk, Wv, bv, out):
             cols = slice(head * D, (head + 1) * D)
             nc.sync.dma_start(out=bv_all[:, cols], in_=bv[cols].partition_broadcast(P))
 
-        load_weight_block("v", 0)
+        nc.vector.memset(bias_rows[:], 0.0)
         load_x(0)
+        nc.sync.dma_start(out=bias_rows[0:n_bias_rows, :], in_=bk.rearrange("(r p) -> r p", p=P))
+        nc.sync.dma_start(out=bias_rows[n_bias_rows : 2 * n_bias_rows, :], in_=bq.rearrange("(r p) -> r p", p=P))
+        nc.sync.dma_start(out=bias_rows[2 * n_bias_rows : n_stage_rows, :], in_=bv[0:D].rearrange("(r p) -> r p", p=P))
+        load_weight_block("v", 0)
         load_weight_block("k", 0)
         load_weight_block("q", 0)
         load_x(1)
         for head in range(1, H):
-            for which in REGROUP_ORDER:
+            for which in ("k", "v", "q"):
                 load_weight_block(which, head)
             load_bv(head)
-
-        nc.vector.memset(bias_rows[:], 0.0)
-        nc.scalar.dma_start(out=bias_rows[0:n_bias_rows, :], in_=bk.rearrange("(r p) -> r p", p=P))
-        nc.scalar.dma_start(out=bias_rows[n_bias_rows : 2 * n_bias_rows, :], in_=bq.rearrange("(r p) -> r p", p=P))
-        nc.scalar.dma_start(out=bias_rows[2 * n_bias_rows : n_stage_rows, :], in_=bv[0:D].rearrange("(r p) -> r p", p=P))
 
         masks.make_identity(nc, identity[:])
         nc.vector.memset(zero_col[:], 0.0)
@@ -138,22 +136,28 @@ def tile_multihead_attention_pa_kernel(tc, x, Wq, bq, Wk, bk, Wv, bv, out):
             cols = slice(first_col, first_col + n_cols)
             return (grouped[head][:, cols, :].rearrange("p c t -> p (c t)"), codes[head][:, cols], scales[head][:, cols])
 
+        turned_x = {}
+
         def transpose_x(batch):
             x_words = x_raw[:].bitcast(F32)
-            grouped_words = x_grouped[:].bitcast(F32)
             for pair in range(TOKEN_TILES // 2):
-                turned = psum.tile([P, 2, 2 * P], F32, tag="misc")
+                turned = psum.tile([P, 2, 2 * P], F32, name="turned_ps", tag="misc")
                 for block in range(2):
                     n = batch * TOKEN_TILES + 2 * pair + block
                     for u in range(2):
                         words = x_words[:, n * HALF_E + u : (n + 1) * HALF_E : 2]
                         nc.tensor.transpose(turned[:, u, block * P : (block + 1) * P], words, identity[:])
+                turned_x[(batch, pair)] = turned
+
+        def empty_x(batch):
+            grouped_words = x_grouped[:].bitcast(F32)
+            for pair in range(TOKEN_TILES // 2):
                 first_token = batch * S + pair * 2 * P
                 nc.scalar.copy(
                     out=grouped_words[:, 2 * first_token : 2 * (first_token + 2 * P)].rearrange(
                         "p (r u) -> p r u", u=2
                     ),
-                    in_=turned[:].rearrange("p u r -> p r u"),
+                    in_=turned_x[(batch, pair)][:].rearrange("p u r -> p r u"),
                 )
 
         def new_grouped(head):
@@ -176,7 +180,7 @@ def tile_multihead_attention_pa_kernel(tc, x, Wq, bq, Wk, bk, Wv, bv, out):
 
         fills = {}
         for head in range(1, H):
-            banks = [(which, first) for which in REGROUP_ORDER for first in range(0, D, BANK_COLS)]
+            banks = [("k", 0), ("v", 0), ("v", BANK_COLS), ("k", BANK_COLS), ("q", 0), ("q", BANK_COLS)]
             for step, (which, first) in enumerate(banks):
                 fills[(head - 1) * TILES_PER_HEAD + FIRST_FILL + step] = (head, which, first)
         filled = {}
@@ -240,11 +244,15 @@ def tile_multihead_attention_pa_kernel(tc, x, Wq, bq, Wk, bk, Wv, bv, out):
                 (x_codes, x_scales), slice(batch * S, (batch + 1) * S),
             )
 
-        def project_k_and_v(t):
+        def project_k(t):
+            if not 0 <= t < N_TILES:
+                return
+            project_features("k", t)
+
+        def project_v(t):
             if not 0 <= t < N_TILES:
                 return
             head, batch, j_tile = place(t)
-            project_features("k", t)
             first = batch * S + j_tile * P
             project(
                 "v", t, (x_codes, x_scales), slice(first, first + P),
@@ -271,7 +279,7 @@ def tile_multihead_attention_pa_kernel(tc, x, Wq, bq, Wk, bk, Wv, bv, out):
             )
             live[("neg_k", t)] = neg_k
 
-        def finish_v_and_multiply(t):
+        def finish_v(t):
             if not 0 <= t < N_TILES:
                 return
             head, batch, j_tile = place(t)
@@ -280,6 +288,10 @@ def tile_multihead_attention_pa_kernel(tc, x, Wq, bq, Wk, bk, Wv, bv, out):
                 out=v_full[:], in0=live[("v", t)][:], in1=bv_all[:, head * D : (head + 1) * D], op=ALU.add
             )
             live[("v_full", t)] = v_full
+
+        def multiply(t):
+            if not 0 <= t < N_TILES:
+                return
             neg_score = work.tile([P, S], F32, name="neg_score", bufs=EXP_LAG + 2)
             nc.gpsimd.tensor_tensor(out=neg_score[:], in0=live[("neg_k", t)][:], in1=live[("v_full", t)][:], op=ALU.mult)
             live[("neg_score", t)] = neg_score
@@ -324,12 +336,13 @@ def tile_multihead_attention_pa_kernel(tc, x, Wq, bq, Wk, bk, Wv, bv, out):
             )
 
         transpose_x(0)
-        bias_cols = psum.tile([P, P], BF16, tag="misc")
+        bias_cols = psum.tile([P, P], BF16, name="bias_ps", tag="q")
         nc.tensor.transpose(bias_cols[:], bias_rows[:], identity_bf[:])
+        empty_x(0)
+        nc.scalar.copy(out=bv0_cols[:], in_=bias_cols[:, 2 * n_bias_rows : n_stage_rows])
         nc.scalar.mul(out=neg_bk[:], in_=bias_cols[:, 0:n_bias_rows], mul=-score_scale)
         nc.scalar.copy(out=bq_cols[:], in_=bias_cols[:, n_bias_rows : 2 * n_bias_rows])
-        nc.scalar.copy(out=bv0_cols[:], in_=bias_cols[:, 2 * n_bias_rows : n_stage_rows])
-        spread = psum.tile([P, D], F32, tag="misc")
+        spread = psum.tile([P, D], F32, name="spread_ps", tag="q")
         for r in range(J_TILES):
             nc.tensor.matmul(
                 out=spread[:, r * P : (r + 1) * P],
@@ -341,31 +354,42 @@ def tile_multihead_attention_pa_kernel(tc, x, Wq, bq, Wk, bk, Wv, bv, out):
         nc.scalar.copy(out=bv_all[:, 0:D], in_=spread[:])
         new_grouped(0)
         regroup(nc.vector.tensor_copy, 0, BLOCK_COL["v"], D)
+        quantise(*x_job(0))
         quantise(*weight_job(0, BLOCK_COL["v"], D))
         regroup(nc.vector.tensor_copy, 0, BLOCK_COL["k"], HALF_D)
-        quantise(*x_job(0))
         quantise(*weight_job(0, BLOCK_COL["k"], HALF_D))
-        head0_rest = [BLOCK_COL["k"] + HALF_D, BLOCK_COL["q"], BLOCK_COL["q"] + HALF_D]
+        project_v(0)
+        project_k(0)
+        project_k(1)
+        head0_rest = {-1: BLOCK_COL["k"] + HALF_D, 0: BLOCK_COL["q"], 2: BLOCK_COL["q"] + HALF_D}
 
-        for period in range(-1, last_period):
-            project_q(period - SUM_LAG + 1)
-            project_k_and_v(period + 1)
-            fill_bank(period)
-            finish_k(period)
-            if period == 0:
-                transpose_x(1)
-                to_quantise[2].append(x_job(1))
-            if 0 <= period < len(head0_rest):
-                regroup(nc.vector.tensor_copy, 0, head0_rest[period], HALF_D)
-                to_quantise[period].append(weight_job(0, head0_rest[period], HALF_D))
-            empty_bank(period)
-            row_maximum(period - MAX_LAG)
-            exponentials(period - EXP_LAG)
-            weighted_sum(period - SUM_LAG)
+        for period in range(-1, N_TILES + SUM_LAG):
+            finish_v(period)
+            multiply(period)
             if period >= 0:
                 for job in to_quantise[period]:
                     quantise(*job)
-            finish_v_and_multiply(period)
+            row_maximum(period - MAX_LAG)
+            exponentials(period - EXP_LAG)
+            if period in head0_rest and period < 0:
+                regroup(nc.scalar.copy, 0, head0_rest[period], HALF_D)
+                to_quantise[period + 1].append(weight_job(0, head0_rest[period], HALF_D))
+            finish_k(period + 1)
+            if period in head0_rest and period >= 0:
+                regroup(nc.scalar.copy, 0, head0_rest[period], HALF_D)
+                to_quantise[period + 1].append(weight_job(0, head0_rest[period], HALF_D))
+            if period == 1:
+                empty_x(1)
+                to_quantise[2].append(x_job(1))
+            empty_bank(period)
+            weighted_sum(period - SUM_LAG)
+            if period >= 0:
+                project_q(period - 1)
+                project_v(period + 1)
+                project_k(period + 2)
+            if period == 0:
+                transpose_x(1)
+            fill_bank(period)
 
         nc.vector.reciprocal(out=reciprocal[:], in_=denominator[:])
         nc.vector.tensor_tensor(out=result[:, 0:N_TILES], in0=numerator[:], in1=reciprocal[:], op=ALU.mult)

@@ -31,11 +31,15 @@ HALF_D = D // 2
 RUN = 4
 BANK_COLS = 256
 MM_COLS = 128
-FIRST_FILL = 2
+SCALE_BV = 5
+FIRST_FILL = 0
+QUANT_STEP = {"k": 4, "v": 6, "q": 8}
 
 MAX_LAG = 1
 EXP_LAG = 2
-SUM_LAG = 2
+SUM_LAG = 3
+
+DIRECT_TILES = (0, N_TILES - 1)
 
 FLOPS = 2 * B * S * E * 3 * H * D
 
@@ -71,10 +75,11 @@ def tile_multihead_attention_pa_kernel(tc, x, Wq, bq, Wk, bk, Wv, bv, out):
         identity_bf = keep.tile([P, P], BF16)
         n_stage_rows = 2 * n_bias_rows + J_TILES
         bias_rows = keep.tile([P, P], BF16)
-        neg_bk = keep.tile([P, n_bias_rows], F32)
+        bk_cols = keep.tile([P, n_bias_rows], F32)
         bq_cols = keep.tile([P, n_bias_rows], F32)
         bv0_cols = keep.tile([P, J_TILES], BF16)
         bv_all = keep.tile([P, H * D], BF16)
+        neg_bv = keep.tile([P, H * D], F32)
         zero_col = keep.tile([P, 1], F32)
         table_warm = keep.tile([P, 1], F32)
         neg_max = keep.tile([P, N_TILES], F32)
@@ -83,14 +88,15 @@ def tile_multihead_attention_pa_kernel(tc, x, Wq, bq, Wk, bk, Wv, bv, out):
         reciprocal = keep.tile([P, N_TILES], F32)
         result = keep.tile([P, P], F32)
         result_rows = keep.tile([N_TILES, P], F32)
-        products = keep.tile([P, S], F32)
 
-        def load_x(batch):
-            first = batch * TOKEN_TILES * E
-            nc.sync.dma_start(
-                out=x_raw[:, first : first + TOKEN_TILES * E].rearrange("p (n e) -> p n e", e=E),
-                in_=x[batch].rearrange("(n p) e -> p n e", p=P),
-            )
+        def load_x(batch, n_parts):
+            tiles = TOKEN_TILES // n_parts
+            for part in range(n_parts):
+                first = batch * TOKEN_TILES + part * tiles
+                nc.sync.dma_start(
+                    out=x_raw[:, first * E : (first + tiles) * E].rearrange("p (n e) -> p n e", e=E),
+                    in_=x[batch, part * tiles * P : (part + 1) * tiles * P, :].rearrange("(n p) e -> p n e", p=P),
+                )
 
         def load_weight_block(which, head):
             nc.sync.dma_start(
@@ -103,14 +109,14 @@ def tile_multihead_attention_pa_kernel(tc, x, Wq, bq, Wk, bk, Wv, bv, out):
             nc.sync.dma_start(out=bv_all[:, cols], in_=bv[cols].partition_broadcast(P))
 
         nc.vector.memset(bias_rows[:], 0.0)
-        load_x(0)
+        load_x(0, 2)
         nc.sync.dma_start(out=bias_rows[0:n_bias_rows, :], in_=bk.rearrange("(r p) -> r p", p=P))
         nc.sync.dma_start(out=bias_rows[n_bias_rows : 2 * n_bias_rows, :], in_=bq.rearrange("(r p) -> r p", p=P))
         nc.sync.dma_start(out=bias_rows[2 * n_bias_rows : n_stage_rows, :], in_=bv[0:D].rearrange("(r p) -> r p", p=P))
         load_weight_block("v", 0)
         load_weight_block("k", 0)
         load_weight_block("q", 0)
-        load_x(1)
+        load_x(1, 1)
         for head in range(1, H):
             for which in ("k", "v", "q"):
                 load_weight_block(which, head)
@@ -138,10 +144,10 @@ def tile_multihead_attention_pa_kernel(tc, x, Wq, bq, Wk, bk, Wv, bv, out):
 
         turned_x = {}
 
-        def transpose_x(batch):
+        def transpose_x(batch, tag):
             x_words = x_raw[:].bitcast(F32)
             for pair in range(TOKEN_TILES // 2):
-                turned = psum.tile([P, 2, 2 * P], F32, name="turned_ps", tag="misc")
+                turned = psum.tile([P, 2, 2 * P], F32, name="turned_ps", tag=tag)
                 for block in range(2):
                     n = batch * TOKEN_TILES + 2 * pair + block
                     for u in range(2):
@@ -175,14 +181,17 @@ def tile_multihead_attention_pa_kernel(tc, x, Wq, bq, Wk, bk, Wv, bv, out):
                         ),
                     )
 
-        last_period = N_TILES + SUM_LAG
-        to_quantise = {n: [] for n in range(last_period)}
+        last_period = N_TILES + SUM_LAG - 1
+        to_quantise = {n: [] for n in range(last_period + 1)}
+        to_quantise[2].append("x")
 
         fills = {}
         for head in range(1, H):
-            banks = [("k", 0), ("v", 0), ("v", BANK_COLS), ("k", BANK_COLS), ("q", 0), ("q", BANK_COLS)]
+            banks = [(which, first) for which in BLOCKS for first in range(0, D, BANK_COLS)]
             for step, (which, first) in enumerate(banks):
                 fills[(head - 1) * TILES_PER_HEAD + FIRST_FILL + step] = (head, which, first)
+            for which, step in QUANT_STEP.items():
+                to_quantise[(head - 1) * TILES_PER_HEAD + step].append((head, BLOCK_COL[which], D))
         filled = {}
 
         def fill_bank(period):
@@ -210,7 +219,6 @@ def tile_multihead_attention_pa_kernel(tc, x, Wq, bq, Wk, bk, Wv, bv, out):
             words = grouped[head][:].rearrange("p c t -> p (c t)").bitcast(F32)
             half = PACK // 2
             nc.scalar.copy(out=words[:, lo * half : (lo + BANK_COLS) * half], in_=filled[period - 1][:].bitcast(F32))
-            to_quantise[period + 1].append(weight_job(head, lo, BANK_COLS))
 
         live = {}
 
@@ -265,35 +273,54 @@ def tile_multihead_attention_pa_kernel(tc, x, Wq, bq, Wk, bk, Wv, bv, out):
             project_features("q", t)
 
         def finish_k(t):
-            if not 0 <= t < N_TILES:
+            if not 0 <= t < N_TILES or t in DIRECT_TILES:
                 return
             head, batch, j_tile = place(t)
             bias_col = head * J_TILES + j_tile
-            neg_k = work.tile([P, S], F32, name="neg_k")
+            k_full = work.tile([P, S], F32, name="k_full")
             nc.scalar.activation(
-                out=neg_k[:],
-                in_=live[("k", t)][:],
-                func=ACT.Identity,
-                bias=neg_bk[:, bias_col : bias_col + 1],
-                scale=-score_scale,
+                out=k_full[:], in_=live[("k", t)][:], func=ACT.Identity, bias=bk_cols[:, bias_col : bias_col + 1]
             )
-            live[("neg_k", t)] = neg_k
+            live[("k_full", t)] = k_full
+
+        def scale_bv(head):
+            cols = slice(head * D, (head + 1) * D)
+            nc.scalar.mul(out=neg_bv[:, cols], in_=bv_all[:, cols], mul=-score_scale)
 
         def finish_v(t):
             if not 0 <= t < N_TILES:
                 return
             head, batch, j_tile = place(t)
-            v_full = work.tile([P, S], F32, name="v_full")
-            nc.vector.tensor_tensor(
-                out=v_full[:], in0=live[("v", t)][:], in1=bv_all[:, head * D : (head + 1) * D], op=ALU.add
+            neg_v = work.tile([P, S], F32, name="neg_v")
+            nc.vector.scalar_tensor_tensor(
+                out=neg_v[:],
+                in0=live[("v", t)][:],
+                scalar=-score_scale,
+                in1=neg_bv[:, head * D : (head + 1) * D],
+                op0=ALU.mult,
+                op1=ALU.add,
             )
-            live[("v_full", t)] = v_full
+            live[("neg_v", t)] = neg_v
 
-        def multiply(t):
-            if not 0 <= t < N_TILES:
+        def multiply(t, direct):
+            if not 0 <= t < N_TILES or direct != (t in DIRECT_TILES):
                 return
             neg_score = work.tile([P, S], F32, name="neg_score", bufs=EXP_LAG + 2)
-            nc.gpsimd.tensor_tensor(out=neg_score[:], in0=live[("neg_k", t)][:], in1=live[("v_full", t)][:], op=ALU.mult)
+            if direct:
+                head, batch, j_tile = place(t)
+                bias_col = head * J_TILES + j_tile
+                nc.vector.scalar_tensor_tensor(
+                    out=neg_score[:],
+                    in0=live[("k", t)][:],
+                    scalar=bk_cols[:, bias_col : bias_col + 1],
+                    in1=live[("neg_v", t)][:],
+                    op0=ALU.add,
+                    op1=ALU.mult,
+                )
+            else:
+                nc.gpsimd.tensor_tensor(
+                    out=neg_score[:], in0=live[("k_full", t)][:], in1=live[("neg_v", t)][:], op=ALU.mult
+                )
             live[("neg_score", t)] = neg_score
 
         def row_maximum(t):
@@ -325,6 +352,7 @@ def tile_multihead_attention_pa_kernel(tc, x, Wq, bq, Wk, bk, Wv, bv, out):
             head, batch, j_tile = place(t)
             bias_col = head * J_TILES + j_tile
             col = out_row(t)
+            products = work.tile([P, S], F32, name="products")
             nc.vector.scalar_tensor_tensor(
                 out=products[:],
                 in0=live[("q", t)][:],
@@ -335,12 +363,12 @@ def tile_multihead_attention_pa_kernel(tc, x, Wq, bq, Wk, bk, Wv, bv, out):
                 accum_out=numerator[:, col : col + 1],
             )
 
-        transpose_x(0)
+        transpose_x(0, "misc")
         bias_cols = psum.tile([P, P], BF16, name="bias_ps", tag="q")
         nc.tensor.transpose(bias_cols[:], bias_rows[:], identity_bf[:])
         empty_x(0)
         nc.scalar.copy(out=bv0_cols[:], in_=bias_cols[:, 2 * n_bias_rows : n_stage_rows])
-        nc.scalar.mul(out=neg_bk[:], in_=bias_cols[:, 0:n_bias_rows], mul=-score_scale)
+        nc.scalar.copy(out=bk_cols[:], in_=bias_cols[:, 0:n_bias_rows])
         nc.scalar.copy(out=bq_cols[:], in_=bias_cols[:, n_bias_rows : 2 * n_bias_rows])
         spread = psum.tile([P, D], F32, name="spread_ps", tag="q")
         for r in range(J_TILES):
@@ -351,47 +379,66 @@ def tile_multihead_attention_pa_kernel(tc, x, Wq, bq, Wk, bk, Wv, bv, out):
                 start=True,
                 stop=True,
             )
-        nc.scalar.copy(out=bv_all[:, 0:D], in_=spread[:])
+        nc.scalar.mul(out=neg_bv[:, 0:D], in_=spread[:], mul=-score_scale)
         new_grouped(0)
         regroup(nc.vector.tensor_copy, 0, BLOCK_COL["v"], D)
         quantise(*x_job(0))
         quantise(*weight_job(0, BLOCK_COL["v"], D))
-        regroup(nc.vector.tensor_copy, 0, BLOCK_COL["k"], HALF_D)
-        quantise(*weight_job(0, BLOCK_COL["k"], HALF_D))
+        for copy, first_col in ((nc.vector.tensor_copy, 0), (nc.scalar.copy, P)):
+            regroup(copy, 0, BLOCK_COL["k"] + first_col, P)
+            quantise(*weight_job(0, BLOCK_COL["k"] + first_col, P))
         project_v(0)
         project_k(0)
-        project_k(1)
-        head0_rest = {-1: BLOCK_COL["k"] + HALF_D, 0: BLOCK_COL["q"], 2: BLOCK_COL["q"] + HALF_D}
+        head0_rest = {
+            -1: (nc.scalar.copy, BLOCK_COL["k"] + HALF_D, 0),
+            0: (nc.vector.tensor_copy, BLOCK_COL["q"], 1),
+            2: (nc.scalar.copy, BLOCK_COL["q"] + HALF_D, 4),
+        }
+        for engine_copy, first_col, when in head0_rest.values():
+            to_quantise[when].append((0, first_col, HALF_D))
 
-        for period in range(-1, N_TILES + SUM_LAG):
+        def regroup_head0(period):
+            if period in head0_rest:
+                regroup(head0_rest[period][0], 0, head0_rest[period][1], HALF_D)
+
+        for period in range(-1, last_period + 1):
             finish_v(period)
-            multiply(period)
+            multiply(period, False)
+            if period == 0:
+                multiply(period, True)
             if period >= 0:
                 for job in to_quantise[period]:
-                    quantise(*job)
-            row_maximum(period - MAX_LAG)
+                    quantise(*(x_job(1) if job == "x" else weight_job(*job)))
+            if period == last_period:
+                nc.vector.reciprocal(out=reciprocal[:], in_=denominator[:])
+            if period == N_TILES:
+                row_maximum(period - MAX_LAG)
+            weighted_sum(period - SUM_LAG)
+            if period > 0:
+                multiply(period, True)
+            if period < N_TILES:
+                row_maximum(period - MAX_LAG)
             exponentials(period - EXP_LAG)
-            if period in head0_rest and period < 0:
-                regroup(nc.scalar.copy, 0, head0_rest[period], HALF_D)
-                to_quantise[period + 1].append(weight_job(0, head0_rest[period], HALF_D))
+            if period < 0:
+                regroup_head0(period)
             finish_k(period + 1)
-            if period in head0_rest and period >= 0:
-                regroup(nc.scalar.copy, 0, head0_rest[period], HALF_D)
-                to_quantise[period + 1].append(weight_job(0, head0_rest[period], HALF_D))
+            if period >= 0:
+                regroup_head0(period)
             if period == 1:
                 empty_x(1)
-                to_quantise[2].append(x_job(1))
+            if period % TILES_PER_HEAD == SCALE_BV and period // TILES_PER_HEAD + 1 < H:
+                scale_bv(period // TILES_PER_HEAD + 1)
             empty_bank(period)
-            weighted_sum(period - SUM_LAG)
+            project_q(period - SUM_LAG + 1)
+            project_v(period + 2)
             if period >= 0:
-                project_q(period - 1)
-                project_v(period + 1)
                 project_k(period + 2)
+            else:
+                project_k(1)
             if period == 0:
-                transpose_x(1)
+                transpose_x(1, "q")
             fill_bank(period)
 
-        nc.vector.reciprocal(out=reciprocal[:], in_=denominator[:])
         nc.vector.tensor_tensor(out=result[:, 0:N_TILES], in0=numerator[:], in1=reciprocal[:], op=ALU.mult)
         turned_result = psum.tile([P, P], F32, tag="misc")
         nc.tensor.transpose(turned_result[:], result[:], identity[:])

@@ -28,6 +28,8 @@ BLOCK_COL = {"k": 0, "v": D, "q": 2 * D}
 HEAD_COLS = 3 * D
 HALF_D = D // 2
 
+BLOCK = 32
+assert N_TILES == BLOCK
 RUN = 4
 BANK_COLS = 256
 MM_COLS = 128
@@ -40,6 +42,8 @@ EXP_LAG = 2
 SUM_LAG = 3
 
 DIRECT_TILES = (0, N_TILES - 1)
+
+TURNED_TILES = (26, 27)
 
 FLOPS = 2 * B * S * E * 3 * H * D
 
@@ -73,11 +77,13 @@ def tile_multihead_attention_pa_kernel(tc, x, Wq, bq, Wk, bk, Wv, bv, out):
 
         identity = keep.tile([P, P], F32)
         identity_bf = keep.tile([P, P], BF16)
-        n_stage_rows = 2 * n_bias_rows + J_TILES
+        n_stage_rows = 3 * n_bias_rows
         bias_rows = keep.tile([P, P], BF16)
         bk_cols = keep.tile([P, n_bias_rows], F32)
         bq_cols = keep.tile([P, n_bias_rows], F32)
         bv0_cols = keep.tile([P, J_TILES], BF16)
+        neg_bv_cols = keep.tile([P, J_TILES], F32)
+        v_turned = keep.tile([P, J_TILES, 2 * P], F32)
         bv_all = keep.tile([P, H * D], BF16)
         neg_bv = keep.tile([P, H * D], F32)
         zero_col = keep.tile([P, 1], F32)
@@ -86,8 +92,8 @@ def tile_multihead_attention_pa_kernel(tc, x, Wq, bq, Wk, bk, Wv, bv, out):
         denominator = keep.tile([P, N_TILES], F32)
         numerator = keep.tile([P, N_TILES], F32)
         reciprocal = keep.tile([P, N_TILES], F32)
-        result = keep.tile([P, P], F32)
-        result_rows = keep.tile([N_TILES, P], F32)
+        result = keep.tile([P, N_TILES], F32, align_bytes=64)
+        result_rows = keep.tile([P, N_TILES], F32, align_bytes=64)
 
         def load_x(batch, n_parts):
             tiles = TOKEN_TILES // n_parts
@@ -112,7 +118,7 @@ def tile_multihead_attention_pa_kernel(tc, x, Wq, bq, Wk, bk, Wv, bv, out):
         load_x(0, 2)
         nc.sync.dma_start(out=bias_rows[0:n_bias_rows, :], in_=bk.rearrange("(r p) -> r p", p=P))
         nc.sync.dma_start(out=bias_rows[n_bias_rows : 2 * n_bias_rows, :], in_=bq.rearrange("(r p) -> r p", p=P))
-        nc.sync.dma_start(out=bias_rows[2 * n_bias_rows : n_stage_rows, :], in_=bv[0:D].rearrange("(r p) -> r p", p=P))
+        nc.sync.dma_start(out=bias_rows[2 * n_bias_rows : n_stage_rows, :], in_=bv.rearrange("(r p) -> r p", p=P))
         load_weight_block("v", 0)
         load_weight_block("k", 0)
         load_weight_block("q", 0)
@@ -124,7 +130,6 @@ def tile_multihead_attention_pa_kernel(tc, x, Wq, bq, Wk, bk, Wv, bv, out):
 
         masks.make_identity(nc, identity[:])
         nc.vector.memset(zero_col[:], 0.0)
-        nc.vector.memset(result[:], 0.0)
         nc.vector.tensor_copy(out=identity_bf[:], in_=identity[:])
         nc.scalar.activation(out=table_warm[:], in_=zero_col[:], func=ACT.Exp)
 
@@ -257,8 +262,49 @@ def tile_multihead_attention_pa_kernel(tc, x, Wq, bq, Wk, bk, Wv, bv, out):
                 return
             project_features("k", t)
 
+        def project_turned_v():
+            head, batch, j_tile = place(TURNED_TILES[0])
+            first = batch * S + j_tile * P
+            for half in range(2):
+                bank = psum.tile([P, 2, 2 * P], F32, name="turned_v_ps", tag="misc")
+                for r in range(2):
+                    first_col = BLOCK_COL["v"] + (2 * half + r) * P
+                    nc.tensor.matmul_mx(
+                        out=bank[:, r, :],
+                        lhsT=codes[head][:, first_col : first_col + P].bitcast(FP8X4),
+                        lhsT_scale=scales[head][:, first_col : first_col + P],
+                        rhs=x_codes[:, first : first + 2 * P].bitcast(FP8X4),
+                        rhs_scale=x_scales[:, first : first + 2 * P],
+                        start=True,
+                        stop=True,
+                    )
+                live[("turned_v", half)] = bank
+
+        def finish_turned_v(half):
+            for r in range(2):
+                block = 2 * half + r
+                nc.scalar.activation(
+                    out=v_turned[:, block, :],
+                    in_=live[("turned_v", half)][:, r, :],
+                    func=ACT.Identity,
+                    bias=neg_bv_cols[:, block : block + 1],
+                    scale=-score_scale,
+                )
+
+        def turn_back(t):
+            bank = psum.tile([P, S], F32, name="v_ps", tag="v")
+            first = (t - TURNED_TILES[0]) * P
+            for block in range(J_TILES):
+                nc.tensor.transpose(
+                    bank[:, block * P : (block + 1) * P], v_turned[:, block, first : first + P], identity[:]
+                )
+            live[("v", t)] = bank
+
         def project_v(t):
             if not 0 <= t < N_TILES:
+                return
+            if t in TURNED_TILES:
+                turn_back(t)
                 return
             head, batch, j_tile = place(t)
             first = batch * S + j_tile * P
@@ -292,6 +338,10 @@ def tile_multihead_attention_pa_kernel(tc, x, Wq, bq, Wk, bk, Wv, bv, out):
                 return
             head, batch, j_tile = place(t)
             neg_v = work.tile([P, S], F32, name="neg_v")
+            live[("neg_v", t)] = neg_v
+            if t in TURNED_TILES:
+                nc.scalar.copy(out=neg_v[:], in_=live[("v", t)][:])
+                return
             nc.vector.scalar_tensor_tensor(
                 out=neg_v[:],
                 in0=live[("v", t)][:],
@@ -300,7 +350,6 @@ def tile_multihead_attention_pa_kernel(tc, x, Wq, bq, Wk, bk, Wv, bv, out):
                 op0=ALU.mult,
                 op1=ALU.add,
             )
-            live[("neg_v", t)] = neg_v
 
         def multiply(t, direct):
             if not 0 <= t < N_TILES or direct != (t in DIRECT_TILES):
@@ -367,9 +416,10 @@ def tile_multihead_attention_pa_kernel(tc, x, Wq, bq, Wk, bk, Wv, bv, out):
         bias_cols = psum.tile([P, P], BF16, name="bias_ps", tag="q")
         nc.tensor.transpose(bias_cols[:], bias_rows[:], identity_bf[:])
         empty_x(0)
-        nc.scalar.copy(out=bv0_cols[:], in_=bias_cols[:, 2 * n_bias_rows : n_stage_rows])
+        nc.scalar.copy(out=bv0_cols[:], in_=bias_cols[:, 2 * n_bias_rows : 2 * n_bias_rows + J_TILES])
         nc.scalar.copy(out=bk_cols[:], in_=bias_cols[:, 0:n_bias_rows])
         nc.scalar.copy(out=bq_cols[:], in_=bias_cols[:, n_bias_rows : 2 * n_bias_rows])
+        nc.scalar.mul(out=neg_bv_cols[:], in_=bias_cols[:, n_stage_rows - J_TILES : n_stage_rows], mul=-score_scale)
         spread = psum.tile([P, D], F32, name="spread_ps", tag="q")
         for r in range(J_TILES):
             nc.tensor.matmul(
@@ -402,7 +452,8 @@ def tile_multihead_attention_pa_kernel(tc, x, Wq, bq, Wk, bk, Wv, bv, out):
                 regroup(head0_rest[period][0], 0, head0_rest[period][1], HALF_D)
 
         for period in range(-1, last_period + 1):
-            finish_v(period)
+            if period not in TURNED_TILES:
+                finish_v(period)
             multiply(period, False)
             if period == 0:
                 multiply(period, True)
@@ -429,6 +480,13 @@ def tile_multihead_attention_pa_kernel(tc, x, Wq, bq, Wk, bk, Wv, bv, out):
             if period % TILES_PER_HEAD == SCALE_BV and period // TILES_PER_HEAD + 1 < H:
                 scale_bv(period // TILES_PER_HEAD + 1)
             empty_bank(period)
+            if period + 1 in TURNED_TILES:
+                finish_v(period + 1)
+            if period == TURNED_TILES[0] - 3:
+                project_turned_v()
+                finish_turned_v(0)
+            if period == TURNED_TILES[0] - 2:
+                finish_turned_v(1)
             project_q(period - SUM_LAG + 1)
             project_v(period + 2)
             if period >= 0:
@@ -439,8 +497,9 @@ def tile_multihead_attention_pa_kernel(tc, x, Wq, bq, Wk, bk, Wv, bv, out):
                 transpose_x(1, "q")
             fill_bank(period)
 
-        nc.vector.tensor_tensor(out=result[:, 0:N_TILES], in0=numerator[:], in1=reciprocal[:], op=ALU.mult)
-        turned_result = psum.tile([P, P], F32, tag="misc")
-        nc.tensor.transpose(turned_result[:], result[:], identity[:])
-        nc.scalar.copy(out=result_rows[:], in_=turned_result[0:N_TILES, :])
-        nc.sync.dma_start(out=out.rearrange("b h (n p) -> (b h n) p", p=P), in_=result_rows[:])
+        nc.vector.tensor_tensor(out=result[:], in0=numerator[:], in1=reciprocal[:], op=ALU.mult)
+        nc.vector.transpose(out=result_rows[:], in_=result[:])
+        rows_of_out = out.rearrange("b h (n q w) -> q (b h n) w", q=P // BLOCK, w=BLOCK)
+        for q in range(P // BLOCK):
+            queue = nc.sync if q % 2 == 0 else nc.scalar
+            queue.dma_start(out=rows_of_out[q], in_=result_rows[q * BLOCK : (q + 1) * BLOCK, :])

@@ -33,7 +33,8 @@ assert N_TILES == BLOCK
 RUN = 4
 BANK_COLS = 256
 MM_COLS = 128
-SCALE_BV = 5
+SCALED_V = (0, H - 1)
+SCALE_BV = 15
 FIRST_FILL = 0
 QUANT_STEP = {"k": 4, "v": 6, "q": 8}
 
@@ -80,6 +81,7 @@ def tile_multihead_attention_pa_kernel(tc, x, Wq, bq, Wk, bk, Wv, bv, out):
         n_stage_rows = 3 * n_bias_rows
         bias_rows = keep.tile([P, P], BF16)
         bk_cols = keep.tile([P, n_bias_rows], F32)
+        neg_bk = keep.tile([P, n_bias_rows], F32)
         bq_cols = keep.tile([P, n_bias_rows], F32)
         bv0_cols = keep.tile([P, J_TILES], BF16)
         neg_bv_cols = keep.tile([P, J_TILES], F32)
@@ -121,8 +123,8 @@ def tile_multihead_attention_pa_kernel(tc, x, Wq, bq, Wk, bk, Wv, bv, out):
         nc.sync.dma_start(out=bias_rows[2 * n_bias_rows : n_stage_rows, :], in_=bv.rearrange("(r p) -> r p", p=P))
         load_weight_block("v", 0)
         load_weight_block("k", 0)
-        load_weight_block("q", 0)
         load_x(1, 1)
+        load_weight_block("q", 0)
         for head in range(1, H):
             for which in ("k", "v", "q"):
                 load_weight_block(which, head)
@@ -173,6 +175,9 @@ def tile_multihead_attention_pa_kernel(tc, x, Wq, bq, Wk, bk, Wv, bv, out):
 
         def new_grouped(head):
             grouped[head] = group_pool.tile([P, HEAD_COLS, PACK], BF16, name="grouped", align_bytes=64)
+
+        def gpsimd_copy(out, in_):
+            nc.gpsimd.tensor_scalar(out=out, in0=in_, scalar1=1.0, scalar2=0.0, op0=ALU.mult, op1=ALU.add)
 
         def regroup(copy, head, first_col, n_cols):
             for block, which in enumerate(BLOCKS):
@@ -323,9 +328,14 @@ def tile_multihead_attention_pa_kernel(tc, x, Wq, bq, Wk, bk, Wv, bv, out):
                 return
             head, batch, j_tile = place(t)
             bias_col = head * J_TILES + j_tile
+            bias = bk_cols if head in SCALED_V else neg_bk
             k_full = work.tile([P, S], F32, name="k_full")
             nc.scalar.activation(
-                out=k_full[:], in_=live[("k", t)][:], func=ACT.Identity, bias=bk_cols[:, bias_col : bias_col + 1]
+                out=k_full[:],
+                in_=live[("k", t)][:],
+                func=ACT.Identity,
+                bias=bias[:, bias_col : bias_col + 1],
+                scale=1.0 if head in SCALED_V else -score_scale,
             )
             live[("k_full", t)] = k_full
 
@@ -337,19 +347,19 @@ def tile_multihead_attention_pa_kernel(tc, x, Wq, bq, Wk, bk, Wv, bv, out):
             if not 0 <= t < N_TILES:
                 return
             head, batch, j_tile = place(t)
-            neg_v = work.tile([P, S], F32, name="neg_v")
-            live[("neg_v", t)] = neg_v
+            v_full = work.tile([P, S], F32, name="v_full")
+            live[("v_full", t)] = v_full
             if t in TURNED_TILES:
-                nc.scalar.copy(out=neg_v[:], in_=live[("v", t)][:])
+                nc.scalar.copy(out=v_full[:], in_=live[("v", t)][:])
                 return
-            nc.vector.scalar_tensor_tensor(
-                out=neg_v[:],
-                in0=live[("v", t)][:],
-                scalar=-score_scale,
-                in1=neg_bv[:, head * D : (head + 1) * D],
-                op0=ALU.mult,
-                op1=ALU.add,
-            )
+            cols = slice(head * D, (head + 1) * D)
+            if head in SCALED_V:
+                nc.vector.scalar_tensor_tensor(
+                    out=v_full[:], in0=live[("v", t)][:], scalar=-score_scale, in1=neg_bv[:, cols], op0=ALU.mult, op1=ALU.add
+                )
+            else:
+                nc.vector.tensor_tensor(out=v_full[:], in0=live[("v", t)][:], in1=bv_all[:, cols], op=ALU.add)
+            live[("v_full", t)] = v_full
 
         def multiply(t, direct):
             if not 0 <= t < N_TILES or direct != (t in DIRECT_TILES):
@@ -362,13 +372,13 @@ def tile_multihead_attention_pa_kernel(tc, x, Wq, bq, Wk, bk, Wv, bv, out):
                     out=neg_score[:],
                     in0=live[("k", t)][:],
                     scalar=bk_cols[:, bias_col : bias_col + 1],
-                    in1=live[("neg_v", t)][:],
+                    in1=live[("v_full", t)][:],
                     op0=ALU.add,
                     op1=ALU.mult,
                 )
             else:
                 nc.gpsimd.tensor_tensor(
-                    out=neg_score[:], in0=live[("k_full", t)][:], in1=live[("neg_v", t)][:], op=ALU.mult
+                    out=neg_score[:], in0=live[("k_full", t)][:], in1=live[("v_full", t)][:], op=ALU.mult
                 )
             live[("neg_score", t)] = neg_score
 
@@ -418,6 +428,7 @@ def tile_multihead_attention_pa_kernel(tc, x, Wq, bq, Wk, bk, Wv, bv, out):
         empty_x(0)
         nc.scalar.copy(out=bv0_cols[:], in_=bias_cols[:, 2 * n_bias_rows : 2 * n_bias_rows + J_TILES])
         nc.scalar.copy(out=bk_cols[:], in_=bias_cols[:, 0:n_bias_rows])
+        nc.scalar.mul(out=neg_bk[:], in_=bias_cols[:, 0:n_bias_rows], mul=-score_scale)
         nc.scalar.copy(out=bq_cols[:], in_=bias_cols[:, n_bias_rows : 2 * n_bias_rows])
         nc.scalar.mul(out=neg_bv_cols[:], in_=bias_cols[:, n_stage_rows - J_TILES : n_stage_rows], mul=-score_scale)
         spread = psum.tile([P, D], F32, name="spread_ps", tag="q")
@@ -440,8 +451,8 @@ def tile_multihead_attention_pa_kernel(tc, x, Wq, bq, Wk, bk, Wv, bv, out):
         project_v(0)
         project_k(0)
         head0_rest = {
-            -1: (nc.scalar.copy, BLOCK_COL["k"] + HALF_D, 0),
-            0: (nc.vector.tensor_copy, BLOCK_COL["q"], 1),
+            -2: (nc.scalar.copy, BLOCK_COL["k"] + HALF_D, 0),
+            -1: (gpsimd_copy, BLOCK_COL["q"], 1),
             2: (nc.scalar.copy, BLOCK_COL["q"] + HALF_D, 4),
         }
         for engine_copy, first_col, when in head0_rest.values():
@@ -452,11 +463,12 @@ def tile_multihead_attention_pa_kernel(tc, x, Wq, bq, Wk, bk, Wv, bv, out):
                 regroup(head0_rest[period][0], 0, head0_rest[period][1], HALF_D)
 
         for period in range(-1, last_period + 1):
-            if period not in TURNED_TILES:
+            if period not in TURNED_TILES and period != 1:
                 finish_v(period)
             multiply(period, False)
             if period == 0:
                 multiply(period, True)
+                finish_v(1)
             if period >= 0:
                 for job in to_quantise[period]:
                     quantise(*(x_job(1) if job == "x" else weight_job(*job)))
@@ -471,14 +483,15 @@ def tile_multihead_attention_pa_kernel(tc, x, Wq, bq, Wk, bk, Wv, bv, out):
                 row_maximum(period - MAX_LAG)
             exponentials(period - EXP_LAG)
             if period < 0:
-                regroup_head0(period)
+                regroup_head0(-2)
+                regroup_head0(-1)
             finish_k(period + 1)
             if period >= 0:
                 regroup_head0(period)
-            if period == 1:
+            if period == 0:
                 empty_x(1)
-            if period % TILES_PER_HEAD == SCALE_BV and period // TILES_PER_HEAD + 1 < H:
-                scale_bv(period // TILES_PER_HEAD + 1)
+            if period == SCALE_BV:
+                scale_bv(H - 1)
             empty_bank(period)
             if period + 1 in TURNED_TILES:
                 finish_v(period + 1)
@@ -493,7 +506,7 @@ def tile_multihead_attention_pa_kernel(tc, x, Wq, bq, Wk, bk, Wv, bv, out):
                 project_k(period + 2)
             else:
                 project_k(1)
-            if period == 0:
+            if period == -1:
                 transpose_x(1, "q")
             fill_bank(period)
 

@@ -33,8 +33,7 @@ assert N_TILES == BLOCK
 RUN = 4
 BANK_COLS = 256
 MM_COLS = 128
-SCALED_V = (0, H - 1)
-SCALE_BV = 15
+SCALED_V = (0,)
 FIRST_FILL = 0
 QUANT_STEP = {"k": 4, "v": 6, "q": 8}
 
@@ -42,7 +41,7 @@ MAX_LAG = 1
 EXP_LAG = 2
 SUM_LAG = 3
 
-DIRECT_TILES = (0, N_TILES - 1)
+DIRECT_TILES = (0,)
 
 TURNED_TILES = (26, 27)
 
@@ -84,10 +83,10 @@ def tile_multihead_attention_pa_kernel(tc, x, Wq, bq, Wk, bk, Wv, bv, out):
         neg_bk = keep.tile([P, n_bias_rows], F32)
         bq_cols = keep.tile([P, n_bias_rows], F32)
         bv0_cols = keep.tile([P, J_TILES], BF16)
-        neg_bv_cols = keep.tile([P, J_TILES], F32)
+        bv_cols = keep.tile([P, J_TILES], F32)
         v_turned = keep.tile([P, J_TILES, 2 * P], F32)
         bv_all = keep.tile([P, H * D], BF16)
-        neg_bv = keep.tile([P, H * D], F32)
+        neg_bv = keep.tile([P, D], F32)
         zero_col = keep.tile([P, 1], F32)
         table_warm = keep.tile([P, 1], F32)
         neg_max = keep.tile([P, N_TILES], F32)
@@ -292,8 +291,7 @@ def tile_multihead_attention_pa_kernel(tc, x, Wq, bq, Wk, bk, Wv, bv, out):
                     out=v_turned[:, block, :],
                     in_=live[("turned_v", half)][:, r, :],
                     func=ACT.Identity,
-                    bias=neg_bv_cols[:, block : block + 1],
-                    scale=-score_scale,
+                    bias=bv_cols[:, block : block + 1],
                 )
 
         def turn_back(t):
@@ -339,10 +337,6 @@ def tile_multihead_attention_pa_kernel(tc, x, Wq, bq, Wk, bk, Wv, bv, out):
             )
             live[("k_full", t)] = k_full
 
-        def scale_bv(head):
-            cols = slice(head * D, (head + 1) * D)
-            nc.scalar.mul(out=neg_bv[:, cols], in_=bv_all[:, cols], mul=-score_scale)
-
         def finish_v(t):
             if not 0 <= t < N_TILES:
                 return
@@ -355,7 +349,7 @@ def tile_multihead_attention_pa_kernel(tc, x, Wq, bq, Wk, bk, Wv, bv, out):
             cols = slice(head * D, (head + 1) * D)
             if head in SCALED_V:
                 nc.vector.scalar_tensor_tensor(
-                    out=v_full[:], in0=live[("v", t)][:], scalar=-score_scale, in1=neg_bv[:, cols], op0=ALU.mult, op1=ALU.add
+                    out=v_full[:], in0=live[("v", t)][:], scalar=-score_scale, in1=neg_bv[:], op0=ALU.mult, op1=ALU.add
                 )
             else:
                 nc.vector.tensor_tensor(out=v_full[:], in0=live[("v", t)][:], in1=bv_all[:, cols], op=ALU.add)
@@ -430,7 +424,7 @@ def tile_multihead_attention_pa_kernel(tc, x, Wq, bq, Wk, bk, Wv, bv, out):
         nc.scalar.copy(out=bk_cols[:], in_=bias_cols[:, 0:n_bias_rows])
         nc.scalar.mul(out=neg_bk[:], in_=bias_cols[:, 0:n_bias_rows], mul=-score_scale)
         nc.scalar.copy(out=bq_cols[:], in_=bias_cols[:, n_bias_rows : 2 * n_bias_rows])
-        nc.scalar.mul(out=neg_bv_cols[:], in_=bias_cols[:, n_stage_rows - J_TILES : n_stage_rows], mul=-score_scale)
+        nc.scalar.copy(out=bv_cols[:], in_=bias_cols[:, n_stage_rows - J_TILES : n_stage_rows])
         spread = psum.tile([P, D], F32, name="spread_ps", tag="q")
         for r in range(J_TILES):
             nc.tensor.matmul(
@@ -440,7 +434,7 @@ def tile_multihead_attention_pa_kernel(tc, x, Wq, bq, Wk, bk, Wv, bv, out):
                 start=True,
                 stop=True,
             )
-        nc.scalar.mul(out=neg_bv[:, 0:D], in_=spread[:], mul=-score_scale)
+        nc.scalar.mul(out=neg_bv[:], in_=spread[:], mul=-score_scale)
         new_grouped(0)
         regroup(nc.vector.tensor_copy, 0, BLOCK_COL["v"], D)
         quantise(*x_job(0))
@@ -474,13 +468,10 @@ def tile_multihead_attention_pa_kernel(tc, x, Wq, bq, Wk, bk, Wv, bv, out):
                     quantise(*(x_job(1) if job == "x" else weight_job(*job)))
             if period == last_period:
                 nc.vector.reciprocal(out=reciprocal[:], in_=denominator[:])
-            if period == N_TILES:
-                row_maximum(period - MAX_LAG)
             weighted_sum(period - SUM_LAG)
             if period > 0:
                 multiply(period, True)
-            if period < N_TILES:
-                row_maximum(period - MAX_LAG)
+            row_maximum(period - MAX_LAG)
             exponentials(period - EXP_LAG)
             if period < 0:
                 regroup_head0(-2)
@@ -490,8 +481,6 @@ def tile_multihead_attention_pa_kernel(tc, x, Wq, bq, Wk, bk, Wv, bv, out):
                 regroup_head0(period)
             if period == 0:
                 empty_x(1)
-            if period == SCALE_BV:
-                scale_bv(H - 1)
             empty_bank(period)
             if period + 1 in TURNED_TILES:
                 finish_v(period + 1)

from contextlib import ExitStack
import math

import concourse.masks as masks
import concourse.mybir as mybir

BF16 = mybir.dt.bfloat16
F32 = mybir.dt.float32
U32 = mybir.dt.uint32
U8 = mybir.dt.uint8
FP8X4 = mybir.dt.float8_e4m3fn_x4
ALU = mybir.AluOpType
ACT = mybir.ActivationFunctionType

P = 128
PACK = 4
B, S, E, H, D = 2, 512, 512, 4, 512
assert E == P * PACK and S == D

J_TILES = D // P
TILES_PER_HEAD = B * J_TILES
N_TILES = H * TILES_PER_HEAD
TOKEN_TILES = S // P
HALF_E = E // 2

BLOCKS = ("k", "v", "q")
BLOCK_COL = {"k": 0, "v": D, "q": 2 * D}
HEAD_COLS = 3 * D
HALF_D = D // 2

BLOCK = 32
assert N_TILES == BLOCK
RUN = 4
BANK_COLS = 256
MM_COLS = 128
SCALED_V = (0,)
FIRST_FILL = 0
QUANT_STEP = {"k": 4, "v": 6, "q": 8}

MAX_LAG = 1
EXP_LAG = 2
SUM_LAG = 3

DIRECT_TILES = (0,)

TURNED_TILES = (26, 27)

FLOPS = 2 * B * S * E * 3 * H * D


def tile_multihead_attention_pa_kernel(tc, x, Wq, bq, Wk, bk, Wv, bv, out):
    nc = tc.nc
    weights = {"q": Wq, "k": Wk, "v": Wv}
    score_scale = 1.0 / math.sqrt(D)
    n_bias_rows = H * J_TILES

    with ExitStack() as ctx:
        keep = ctx.enter_context(tc.tile_pool(name="keep", bufs=1))
        group_pool = ctx.enter_context(tc.tile_pool(name="group", bufs=2))
        work = ctx.enter_context(tc.tile_pool(name="work", bufs=3))
        psum = ctx.enter_context(tc.psum_pool(name="psum", bufs=2))
        ctx.enter_context(tc.manual_schedule())

        x_raw = keep.tile([P, B * TOKEN_TILES * E], BF16)
        x_grouped = keep.tile([P, B * S * PACK], BF16, align_bytes=64)
        x_codes = keep.tile([P, B * S], U32, align_bytes=64)
        x_scales = keep.tile([P, B * S], U8, align_bytes=64)
        raw = {}
        codes = {}
        scales = {}
        grouped = {}
        for head in range(H):
            for which in BLOCKS:
                raw[(which, head)] = keep.tile([P, PACK, D], BF16, name="raw_%s%d" % (which, head))
            codes[head] = keep.tile([P, HEAD_COLS], U32, name="codes%d" % head, align_bytes=64)
            scales[head] = keep.tile([P, HEAD_COLS], U8, name="scales%d" % head, align_bytes=64)

        identity = keep.tile([P, P], F32)
        identity_bf = keep.tile([P, P], BF16)
        n_stage_rows = 3 * n_bias_rows
        bias_rows = keep.tile([P, P], BF16)
        bk_cols = keep.tile([P, n_bias_rows], F32)
        neg_bk = keep.tile([P, n_bias_rows], F32)
        bq_cols = keep.tile([P, n_bias_rows], F32)
        bv0_cols = keep.tile([P, J_TILES], BF16)
        bv_cols = keep.tile([P, J_TILES], F32)
        v_turned = keep.tile([P, J_TILES, 2 * P], F32)
        bv_all = keep.tile([P, H * D], BF16)
        neg_bv = keep.tile([P, D], F32)
        zero_col = keep.tile([P, 1], F32)
        table_warm = keep.tile([P, 1], F32)
        neg_max = keep.tile([P, N_TILES], F32)
        denominator = keep.tile([P, N_TILES], F32)
        numerator = keep.tile([P, N_TILES], F32)
        reciprocal = keep.tile([P, N_TILES], F32)
        result = keep.tile([P, N_TILES], F32, align_bytes=64)
        result_rows = keep.tile([P, N_TILES], F32, align_bytes=64)

        def load_x(batch, n_parts):
            tiles = TOKEN_TILES // n_parts
            for part in range(n_parts):
                first = batch * TOKEN_TILES + part * tiles
                nc.sync.dma_start(
                    out=x_raw[:, first * E : (first + tiles) * E].rearrange("p (n e) -> p n e", e=E),
                    in_=x[batch, part * tiles * P : (part + 1) * tiles * P, :].rearrange("(n p) e -> p n e", p=P),
                )

        def load_weight_block(which, head):
            nc.sync.dma_start(
                out=raw[(which, head)][:],
                in_=weights[which][:, head * D : (head + 1) * D].rearrange("(p t) c -> p t c", t=PACK),
            )

        def load_bv(head):
            cols = slice(head * D, (head + 1) * D)
            nc.sync.dma_start(out=bv_all[:, cols], in_=bv[cols].partition_broadcast(P))

        nc.vector.memset(bias_rows[:], 0.0)
        load_x(0, 2)
        nc.sync.dma_start(out=bias_rows[0:n_bias_rows, :], in_=bk.rearrange("(r p) -> r p", p=P))
        nc.sync.dma_start(out=bias_rows[n_bias_rows : 2 * n_bias_rows, :], in_=bq.rearrange("(r p) -> r p", p=P))
        nc.sync.dma_start(out=bias_rows[2 * n_bias_rows : n_stage_rows, :], in_=bv.rearrange("(r p) -> r p", p=P))
        load_weight_block("v", 0)
        load_weight_block("k", 0)
        load_x(1, 1)
        load_weight_block("q", 0)
        for head in range(1, H):
            for which in ("k", "v", "q"):
                load_weight_block(which, head)
            load_bv(head)

        masks.make_identity(nc, identity[:])
        nc.vector.memset(zero_col[:], 0.0)
        nc.vector.tensor_copy(out=identity_bf[:], in_=identity[:])
        nc.scalar.activation(out=table_warm[:], in_=zero_col[:], func=ACT.Exp)

        def quantise(in_, codes_out, scales_out):
            nc.vector.quantize_mx(out=codes_out.bitcast(FP8X4), scales=scales_out, in_=in_)

        def x_job(batch):
            return (
                x_grouped[:, batch * S * PACK : (batch + 1) * S * PACK],
                x_codes[:, batch * S : (batch + 1) * S],
                x_scales[:, batch * S : (batch + 1) * S],
            )

        def weight_job(head, first_col, n_cols):
            cols = slice(first_col, first_col + n_cols)
            return (grouped[head][:, cols, :].rearrange("p c t -> p (c t)"), codes[head][:, cols], scales[head][:, cols])

        turned_x = {}

        def transpose_x(batch, tag):
            x_words = x_raw[:].bitcast(F32)
            for pair in range(TOKEN_TILES // 2):
                turned = psum.tile([P, 2, 2 * P], F32, name="turned_ps", tag=tag)
                for block in range(2):
                    n = batch * TOKEN_TILES + 2 * pair + block
                    for u in range(2):
                        words = x_words[:, n * HALF_E + u : (n + 1) * HALF_E : 2]
                        nc.tensor.transpose(turned[:, u, block * P : (block + 1) * P], words, identity[:])
                turned_x[(batch, pair)] = turned

        def empty_x(batch):
            grouped_words = x_grouped[:].bitcast(F32)
            for pair in range(TOKEN_TILES // 2):
                first_token = batch * S + pair * 2 * P
                nc.scalar.copy(
                    out=grouped_words[:, 2 * first_token : 2 * (first_token + 2 * P)].rearrange(
                        "p (r u) -> p r u", u=2
                    ),
                    in_=turned_x[(batch, pair)][:].rearrange("p u r -> p r u"),
                )

        def new_grouped(head):
            grouped[head] = group_pool.tile([P, HEAD_COLS, PACK], BF16, name="grouped", align_bytes=64)

        def gpsimd_copy(out, in_):
            nc.gpsimd.tensor_scalar(out=out, in0=in_, scalar1=1.0, scalar2=0.0, op0=ALU.mult, op1=ALU.add)

        def regroup(copy, head, first_col, n_cols):
            for block, which in enumerate(BLOCKS):
                lo = max(first_col, block * D)
                hi = min(first_col + n_cols, (block + 1) * D)
                if lo < hi:
                    copy(
                        out=grouped[head][:, lo:hi, :].rearrange("p (c i) t -> p c t i", i=RUN),
                        in_=raw[(which, head)][:, :, lo - block * D : hi - block * D].rearrange(
                            "p t (c i) -> p c t i", i=RUN
                        ),
                    )

        last_period = N_TILES + SUM_LAG - 1
        to_quantise = {n: [] for n in range(last_period + 1)}
        to_quantise[2].append("x")

        fills = {}
        for head in range(1, H):
            banks = [(which, first) for which in BLOCKS for first in range(0, D, BANK_COLS)]
            for step, (which, first) in enumerate(banks):
                fills[(head - 1) * TILES_PER_HEAD + FIRST_FILL + step] = (head, which, first)
            for which, step in QUANT_STEP.items():
                to_quantise[(head - 1) * TILES_PER_HEAD + step].append((head, BLOCK_COL[which], D))
        filled = {}

        def fill_bank(period):
            if period not in fills:
                return
            head, which, first = fills[period]
            bank = psum.tile([P, BANK_COLS * PACK], BF16, name="regroup_ps", tag="misc")
            for c in range(0, BANK_COLS, MM_COLS):
                nc.tensor.matmul(
                    out=bank[:, c * PACK : (c + MM_COLS) * PACK].rearrange("p (c t) -> p c t", t=PACK),
                    lhsT=identity_bf[:],
                    rhs=raw[(which, head)][:, :, first + c : first + c + MM_COLS].rearrange("p t c -> p c t"),
                    start=True,
                    stop=True,
                )
            filled[period] = bank

        def empty_bank(period):
            if period - 1 not in fills:
                return
            head, which, first = fills[period - 1]
            if head not in grouped:
                new_grouped(head)
            lo = BLOCK_COL[which] + first
            words = grouped[head][:].rearrange("p c t -> p (c t)").bitcast(F32)
            half = PACK // 2
            nc.scalar.copy(out=words[:, lo * half : (lo + BANK_COLS) * half], in_=filled[period - 1][:].bitcast(F32))

        live = {}

        def place(t):
            head, rest = divmod(t, TILES_PER_HEAD)
            batch, j_tile = divmod(rest, J_TILES)
            return head, batch, j_tile

        def out_row(t):
            head, batch, j_tile = place(t)
            return (batch * H + head) * J_TILES + j_tile

        def project(name, t, stationary, stationary_cols, moving, moving_cols):
            bank = psum.tile([P, S], F32, name=name + "_ps", tag=name)
            nc.tensor.matmul_mx(
                out=bank[:],
                lhsT=stationary[0][:, stationary_cols].bitcast(FP8X4),
                lhsT_scale=stationary[1][:, stationary_cols],
                rhs=moving[0][:, moving_cols].bitcast(FP8X4),
                rhs_scale=moving[1][:, moving_cols],
                start=True,
                stop=True,
            )
            live[(name, t)] = bank

        def project_features(name, t):
            head, batch, j_tile = place(t)
            first = BLOCK_COL[name] + j_tile * P
            project(
                name, t, (codes[head], scales[head]), slice(first, first + P),
                (x_codes, x_scales), slice(batch * S, (batch + 1) * S),
            )

        def project_k(t):
            if not 0 <= t < N_TILES:
                return
            project_features("k", t)

        def project_turned_v():
            head, batch, j_tile = place(TURNED_TILES[0])
            first = batch * S + j_tile * P
            for half in range(2):
                bank = psum.tile([P, 2, 2 * P], F32, name="turned_v_ps", tag="misc")
                for r in range(2):
                    first_col = BLOCK_COL["v"] + (2 * half + r) * P
                    nc.tensor.matmul_mx(
                        out=bank[:, r, :],
                        lhsT=codes[head][:, first_col : first_col + P].bitcast(FP8X4),
                        lhsT_scale=scales[head][:, first_col : first_col + P],
                        rhs=x_codes[:, first : first + 2 * P].bitcast(FP8X4),
                        rhs_scale=x_scales[:, first : first + 2 * P],
                        start=True,
                        stop=True,
                    )
                live[("turned_v", half)] = bank

        def finish_turned_v(half):
            for r in range(2):
                block = 2 * half + r
                nc.scalar.activation(
                    out=v_turned[:, block, :],
                    in_=live[("turned_v", half)][:, r, :],
                    func=ACT.Identity,
                    bias=bv_cols[:, block : block + 1],
                )

        def turn_back(t):
            bank = psum.tile([P, S], F32, name="v_ps", tag="v")
            first = (t - TURNED_TILES[0]) * P
            for block in range(J_TILES):
                nc.tensor.transpose(
                    bank[:, block * P : (block + 1) * P], v_turned[:, block, first : first + P], identity[:]
                )
            live[("v", t)] = bank

        def project_v(t):
            if not 0 <= t < N_TILES:
                return
            if t in TURNED_TILES:
                turn_back(t)
                return
            head, batch, j_tile = place(t)
            first = batch * S + j_tile * P
            project(
                "v", t, (x_codes, x_scales), slice(first, first + P),
                (codes[head], scales[head]), slice(BLOCK_COL["v"], BLOCK_COL["v"] + D),
            )

        def project_q(t):
            if not 0 <= t < N_TILES:
                return
            project_features("q", t)

        def finish_k(t):
            if not 0 <= t < N_TILES or t in DIRECT_TILES:
                return
            head, batch, j_tile = place(t)
            bias_col = head * J_TILES + j_tile
            bias = bk_cols if head in SCALED_V else neg_bk
            k_full = work.tile([P, S], F32, name="k_full")
            nc.scalar.activation(
                out=k_full[:],
                in_=live[("k", t)][:],
                func=ACT.Identity,
                bias=bias[:, bias_col : bias_col + 1],
                scale=1.0 if head in SCALED_V else -score_scale,
            )
            live[("k_full", t)] = k_full

        def finish_v(t):
            if not 0 <= t < N_TILES:
                return
            head, batch, j_tile = place(t)
            v_full = work.tile([P, S], F32, name="v_full")
            live[("v_full", t)] = v_full
            if t in TURNED_TILES:
                nc.scalar.copy(out=v_full[:], in_=live[("v", t)][:])
                return
            cols = slice(head * D, (head + 1) * D)
            if head in SCALED_V:
                nc.vector.scalar_tensor_tensor(
                    out=v_full[:], in0=live[("v", t)][:], scalar=-score_scale, in1=neg_bv[:], op0=ALU.mult, op1=ALU.add
                )
            else:
                nc.vector.tensor_tensor(out=v_full[:], in0=live[("v", t)][:], in1=bv_all[:, cols], op=ALU.add)
            live[("v_full", t)] = v_full

        def multiply(t, direct):
            if not 0 <= t < N_TILES or direct != (t in DIRECT_TILES):
                return
            neg_score = work.tile([P, S], F32, name="neg_score", bufs=EXP_LAG + 2)
            if direct:
                head, batch, j_tile = place(t)
                bias_col = head * J_TILES + j_tile
                nc.vector.scalar_tensor_tensor(
                    out=neg_score[:],
                    in0=live[("k", t)][:],
                    scalar=bk_cols[:, bias_col : bias_col + 1],
                    in1=live[("v_full", t)][:],
                    op0=ALU.add,
                    op1=ALU.mult,
                )
            else:
                nc.gpsimd.tensor_tensor(
                    out=neg_score[:], in0=live[("k_full", t)][:], in1=live[("v_full", t)][:], op=ALU.mult
                )
            live[("neg_score", t)] = neg_score

        def row_maximum(t):
            if not 0 <= t < N_TILES:
                return
            col = out_row(t)
            nc.vector.tensor_reduce(
                out=neg_max[:, col : col + 1], in_=live[("neg_score", t)][:], axis=mybir.AxisListType.X, op=ALU.min
            )

        def exponentials(t):
            if not 0 <= t < N_TILES:
                return
            col = out_row(t)
            weight = work.tile([P, S], F32, name="weight")
            nc.scalar.activation(
                out=weight[:],
                in_=live[("neg_score", t)][:],
                func=ACT.Exp,
                bias=neg_max[:, col : col + 1],
                scale=-1.0,
                accum_out=denominator[:, col : col + 1],
            )
            live[("weight", t)] = weight

        def weighted_sum(t):
            if not 0 <= t < N_TILES:
                return
            head, batch, j_tile = place(t)
            bias_col = head * J_TILES + j_tile
            col = out_row(t)
            products = work.tile([P, S], F32, name="products")
            nc.vector.scalar_tensor_tensor(
                out=products[:],
                in0=live[("q", t)][:],
                scalar=bq_cols[:, bias_col : bias_col + 1],
                in1=live[("weight", t)][:],
                op0=ALU.add,
                op1=ALU.mult,
                accum_out=numerator[:, col : col + 1],
            )

        transpose_x(0, "misc")
        bias_cols = psum.tile([P, P], BF16, name="bias_ps", tag="q")
        nc.tensor.transpose(bias_cols[:], bias_rows[:], identity_bf[:])
        empty_x(0)
        nc.scalar.copy(out=bv0_cols[:], in_=bias_cols[:, 2 * n_bias_rows : 2 * n_bias_rows + J_TILES])
        nc.scalar.copy(out=bk_cols[:], in_=bias_cols[:, 0:n_bias_rows])
        nc.scalar.mul(out=neg_bk[:], in_=bias_cols[:, 0:n_bias_rows], mul=-score_scale)
        nc.scalar.copy(out=bq_cols[:], in_=bias_cols[:, n_bias_rows : 2 * n_bias_rows])
        nc.scalar.copy(out=bv_cols[:], in_=bias_cols[:, n_stage_rows - J_TILES : n_stage_rows])
        spread = psum.tile([P, D], F32, name="spread_ps", tag="q")
        for r in range(J_TILES):
            nc.tensor.matmul(
                out=spread[:, r * P : (r + 1) * P],
                lhsT=bv0_cols[:, r : r + 1].to_broadcast([P, P]),
                rhs=identity_bf[:],
                start=True,
                stop=True,
            )
        nc.scalar.mul(out=neg_bv[:], in_=spread[:], mul=-score_scale)
        new_grouped(0)
        regroup(nc.vector.tensor_copy, 0, BLOCK_COL["v"], D)
        quantise(*x_job(0))
        quantise(*weight_job(0, BLOCK_COL["v"], D))
        for copy, first_col in ((nc.vector.tensor_copy, 0), (nc.scalar.copy, P)):
            regroup(copy, 0, BLOCK_COL["k"] + first_col, P)
            quantise(*weight_job(0, BLOCK_COL["k"] + first_col, P))
        project_v(0)
        project_k(0)
        head0_rest = {
            -2: (nc.scalar.copy, BLOCK_COL["k"] + HALF_D, 0),
            -1: (gpsimd_copy, BLOCK_COL["q"], 1),
            2: (nc.scalar.copy, BLOCK_COL["q"] + HALF_D, 4),
        }
        for engine_copy, first_col, when in head0_rest.values():
            to_quantise[when].append((0, first_col, HALF_D))

        def regroup_head0(period):
            if period in head0_rest:
                regroup(head0_rest[period][0], 0, head0_rest[period][1], HALF_D)

        for period in range(-1, last_period + 1):
            if period not in TURNED_TILES and period != 1:
                finish_v(period)
            multiply(period, False)
            if period == 0:
                multiply(period, True)
                finish_v(1)
            if period >= 0:
                for job in to_quantise[period]:
                    quantise(*(x_job(1) if job == "x" else weight_job(*job)))
            if period == last_period:
                nc.vector.reciprocal(out=reciprocal[:], in_=denominator[:])
            weighted_sum(period - SUM_LAG)
            if period > 0:
                multiply(period, True)
            row_maximum(period - MAX_LAG)
            exponentials(period - EXP_LAG)
            if period < 0:
                regroup_head0(-2)
                regroup_head0(-1)
            finish_k(period + 1)
            if period >= 0:
                regroup_head0(period)
            if period == 0:
                empty_x(1)
            empty_bank(period)
            if period + 1 in TURNED_TILES:
                finish_v(period + 1)
            if period == TURNED_TILES[0] - 3:
                project_turned_v()
                finish_turned_v(0)
            if period == TURNED_TILES[0] - 2:
                finish_turned_v(1)
            project_q(period - SUM_LAG + 1)
            project_v(period + 2)
            if period >= 0:
                project_k(period + 2)
            else:
                project_k(1)
            if period == -1:
                transpose_x(1, "q")
            fill_bank(period)

        nc.vector.tensor_tensor(out=result[:], in0=numerator[:], in1=reciprocal[:], op=ALU.mult)
        nc.vector.transpose(out=result_rows[:], in_=result[:])
        rows_of_out = out.rearrange("b h (n q w) -> q (b h n) w", q=P // BLOCK, w=BLOCK)
        for q in range(P // BLOCK):
            queue = nc.sync if q % 2 == 0 else nc.scalar
            queue.dma_start(out=rows_of_out[q], in_=result_rows[q * BLOCK : (q + 1) * BLOCK, :])
